import numpy as np
import ml_dtypes


def mxq(x, axis, fmt="e4m3"):
    dtype, down = {"e4m3": (ml_dtypes.float8_e4m3fn, 7), "e5m2": (ml_dtypes.float8_e5m2, 14)}[fmt]
    v = np.moveaxis(np.asarray(x, np.float32).astype(ml_dtypes.bfloat16).astype(np.float64), axis, -1)
    blocks = v.reshape(v.shape[:-1] + (-1, 32))
    amax = np.abs(blocks).max(-1, keepdims=True)
    byte = np.maximum(np.where(amax > 0, np.frexp(amax)[1] - 1 + 127, 0) - down, 1)
    scale = np.exp2(byte - 127.0)
    codes = (blocks / scale).astype(np.float32).astype(dtype).astype(np.float64)
    return np.moveaxis((codes * scale).reshape(v.shape), -1, axis)


WIDE = False


def mx_kscale(k):
    if not WIDE:
        return np.ones(k)
    levels = np.array([10, -10, 5, -5, 0])
    if k % 512:
        return np.exp2(np.random.permutation(np.resize(levels, k // 32))).repeat(32)
    a = np.empty((k // 512, 16))
    for p in range(k // 512):
        a[p, :8] = np.random.permutation(np.resize(levels, 8))
        for g in range(8):
            far = levels[np.abs(levels - a[p, g]) >= 10]
            a[p, g + 8] = far[np.random.randint(len(far))]
    return np.exp2(a.ravel()).repeat(32)


BF16 = ml_dtypes.bfloat16


def bf(x):
    return np.asarray(x, np.float32).astype(BF16)


def f64(x):
    return np.asarray(x).astype(np.float64)


B, D, H, F, K = 2048, 1024, 1024, 1024, 128
EPS_LN = 1e-5


def silu(v):
    return v / (1.0 + np.exp(-v))


def setup_inputs():
    s = mx_kscale(D)
    return {"x": bf(np.random.standard_normal((B, D)) * s),
            "W1": bf(np.random.standard_normal((D, H)) / np.sqrt(D) / s[:, None]),
            "b1": bf(0.2 * np.random.standard_normal(H)),
            "g": bf(1.0 + 0.1 * np.random.standard_normal(H)),
            "beta": bf(0.1 * np.random.standard_normal(H))}


def reference(x, W1, b1, g, beta):
    h = silu((mxq(f64(x), 1, "e4m3") @ mxq(f64(W1), 0, "e4m3")) + f64(b1))
    mu = h.mean(-1, keepdims=True)
    var = ((h - mu) ** 2).mean(-1, keepdims=True)
    return (h - mu) / np.sqrt(var + EPS_LN) * f64(g) + f64(beta)

@@ -1,0 +1,228 @@
+from contextlib import ExitStack
+
+import concourse.mybir as mybir
+from concourse.masks import make_identity
+
+F32 = mybir.dt.float32
+BF16 = mybir.dt.bfloat16
+U32 = mybir.dt.uint32
+U8 = mybir.dt.uint8
+I32 = mybir.dt.int32
+FP8X4 = mybir.dt.float8_e4m3fn_x4
+ACT = mybir.ActivationFunctionType
+ALU = mybir.AluOpType
+
+P = 128
+B, D, H = 2048, 1024, 1024
+EPS = 1e-5
+FLOPS = 2 * B * D * H
+NT = B // P
+NJ = H // P
+BANK = 512
+CHUNKS = (2, 2, 2, 2, 2, 2, 2, 2)
+VLIM = 12
+XV = (2,)
+W_VECTOR_COLS = 336
+
+
+def tile_evidentialhead_pa_kernel(tc, x, W1, b1, g, beta, out):
+    nc = tc.nc
+    starts = [sum(CHUNKS[:c]) for c in range(len(CHUNKS))]
+    chunk_of = [c for c, n in enumerate(CHUNKS) for r in range(n)]
+    with ExitStack() as ctx:
+        const = ctx.enter_context(tc.tile_pool(name="const", bufs=1))
+        work = ctx.enter_context(tc.tile_pool(name="work", bufs=2))
+        small = ctx.enter_context(tc.tile_pool(name="small", bufs=6))
+        psum = ctx.enter_context(tc.psum_pool(name="psum", bufs=8))
+
+        def bank(name):
+            return psum.tile([P, BANK], F32, name=name, tag="bank")
+
+        rows = const.tile([P, 2 * H + P], BF16, name="rows")
+        nc.vector.memset(rows[:].bitcast(I32), 0)
+        ones = const.tile([P, P], BF16, name="ones")
+        nc.vector.memset(ones[:], 1.0)
+        neg_half = const.tile([P, 1], F32, name="neg_half")
+        nc.vector.memset(neg_half[:], -0.5)
+        eps_col = const.tile([P, 1], F32, name="eps_col")
+        nc.vector.memset(eps_col[:], EPS)
+        ident = const.tile([P, P], F32, name="ident")
+        make_identity(nc, ident[:])
+        warm = const.tile([P, 1], F32, name="warm")
+        nc.scalar.activation(out=warm[:], in_=neg_half[:], func=ACT.Silu)
+        nc.scalar.dma_start(out=rows[0:1, 0:H], in_=g.unsqueeze(0))
+        nc.scalar.dma_start(out=rows[0:1, H : 2 * H], in_=beta.unsqueeze(0))
+        nc.scalar.dma_start(out=rows[0:NJ, 2 * H : 2 * H + P], in_=b1.rearrange("(j m) -> j m", m=P))
+
+        w_raw = const.tile([P, 8, H], BF16, name="w_raw")
+        for gi in range(2):
+            nc.sync.dma_start(
+                out=w_raw[:, 4 * gi : 4 * gi + 4, :],
+                in_=W1[512 * gi : 512 * gi + 512, :].rearrange("(p e) c -> p e c", e=4),
+            )
+        x_raw = []
+        for c, n in enumerate(CHUNKS):
+            xc = const.tile([P, n, D], BF16, name="x_raw%d" % c)
+            nc.sync.dma_start(
+                out=xc[:], in_=x[P * starts[c] : P * (starts[c] + n), :].rearrange("(p r) k -> p r k", r=n)
+            )
+            x_raw.append(xc)
+
+        b1_rows = const.tile([P, P], F32, name="b1_rows")
+        nc.vector.tensor_copy(out=b1_rows[:], in_=rows[:, 2 * H : 2 * H + P])
+        b1_bank = bank("b1_bank")
+        nc.tensor.transpose(b1_bank[:, 0:P], b1_rows[:], ident[:])
+        b1_col = const.tile([P, NJ], F32, name="b1_col")
+        nc.vector.tensor_copy(out=b1_col[:], in_=b1_bank[:, 0:NJ])
+
+        w_grouped = const.tile([P, 2, H, 4], BF16, name="w_grouped", align_bytes=64)
+        w_codes = const.tile([P, 2, H], U32, name="w_codes", align_bytes=64)
+        w_scales = const.tile([P, 2, H], U8, name="w_scales", align_bytes=64)
+        for gi in range(2):
+            for lo in (0, BANK):
+                cut = lo + W_VECTOR_COLS
+                for copy, a, b in ((nc.vector.tensor_copy, lo, cut), (nc.scalar.copy, cut, lo + BANK)):
+                    copy(
+                        out=w_grouped[:, gi, a:b, :].rearrange("p (c i) t -> p c t i", i=4),
+                        in_=w_raw[:, 4 * gi : 4 * gi + 4, a:b].rearrange("p t (c i) -> p c t i", i=4),
+                    )
+            for lo in (0, BANK):
+                nc.vector.quantize_mx(
+                    out=w_codes[:, gi, lo : lo + BANK].bitcast(FP8X4),
+                    scales=w_scales[:, gi, lo : lo + BANK],
+                    in_=w_grouped[:, gi, lo : lo + BANK, :].rearrange("p c t -> p (c t)"),
+                )
+
+        x_codes = {}
+        x_scales = {}
+
+        def prepare_x(c, copy):
+            n = CHUNKS[c]
+            nb = P * n
+            grouped = work.tile([P, 8 * nb], BF16, name="x_grouped", tag="x_grouped", bufs=3, align_bytes=64)
+            for r in range(n):
+                turned = bank("x_turned")
+                words = x_raw[c][:, r, :].bitcast(F32)
+                for w in range(4):
+                    first = 256 * (w // 2) + w % 2
+                    nc.tensor.transpose(turned[:, P * w : P * w + P], words[:, first : first + 255 : 2], ident[:])
+                copy(
+                    out=grouped[:].bitcast(F32).rearrange("p (g b u) -> p g b u", g=2, u=2)[:, :, P * r : P * r + P, :],
+                    in_=turned[:].rearrange("p (g u b) -> p g b u", g=2, u=2),
+                )
+            x_codes[c] = const.tile([P, 2 * nb], U32, name="x_codes%d" % c, align_bytes=64)
+            x_scales[c] = const.tile([P, 2 * nb], U8, name="x_scales%d" % c, align_bytes=64)
+            nc.vector.quantize_mx(out=x_codes[c][:].bitcast(FP8X4), scales=x_scales[c][:], in_=grouped[:])
+
+        hT = {}
+
+        def produce(c, js):
+            nb = P * CHUNKS[c]
+            for j in js:
+                if j == 0:
+                    hT[c] = work.tile([P, NJ, nb], F32, name="hT", tag="hT", bufs=4)
+                acc = bank("acc")
+                for gi in range(2):
+                    nc.tensor.matmul_mx(
+                        out=acc[:, 0:nb],
+                        lhsT=w_codes[:, gi, P * j : P * j + P].bitcast(FP8X4),
+                        lhsT_scale=w_scales[:, gi, P * j : P * j + P],
+                        rhs=x_codes[c][:, nb * gi : nb * gi + nb].bitcast(FP8X4),
+                        rhs_scale=x_scales[c][:, nb * gi : nb * gi + nb],
+                        start=(gi == 0),
+                        stop=(gi == 1),
+                    )
+                nc.scalar.activation(
+                    out=hT[c][:, j, :], in_=acc[:, 0:nb], func=ACT.Silu, bias=b1_col[:, j : j + 1], scale=1.0
+                )
+
+        gb = const.tile([P, 2 * H], F32, name="gb")
+
+        def spread_g_beta():
+            for q in range(4):
+                spread = bank("spread")
+                nc.tensor.matmul(
+                    out=spread[:], lhsT=ones[:], rhs=rows[:, BANK * q : BANK * q + BANK], start=True, stop=True
+                )
+                nc.vector.tensor_copy(out=gb[:, BANK * q : BANK * q + BANK], in_=spread[:])
+
+        junk = const.tile([P, H], F32, name="junk")
+        centred = {}
+        rstd = {}
+
+        def centre(i):
+            c = chunk_of[i]
+            r = i - starts[c]
+            halves = []
+            for a in range(2):
+                half = bank("h_half")
+                for jj in range(4):
+                    nc.tensor.transpose(half[:, P * jj : P * jj + P], hT[c][:, 4 * a + jj, P * r : P * r + P], ident[:])
+                halves.append(half)
+            t = work.tile([P, H], F32, name="centred", tag="centred", bufs=5)
+            var_eps = small.tile([P, 1], F32, name="var_eps")
+            if (i == 0 or i % 2 == 1) and i < VLIM:
+                stats = small.tile([P, 2, 6], F32, name="stats")
+                for a in range(2):
+                    nc.vector.bn_stats(out=stats[:, a, :], in_=halves[a][:])
+                mean_var = small.tile([P, 2], F32, name="mean_var")
+                nc.vector.bn_aggr(out=mean_var[:], in_=stats[:].rearrange("p a s -> p (a s)"))
+                nc.gpsimd.tensor_scalar(
+                    out=var_eps[:], in0=mean_var[:, 1:2], scalar1=1.0, scalar2=EPS, op0=ALU.mult, op1=ALU.add
+                )
+                for a in range(2):
+                    cols = slice(BANK * a, BANK * a + BANK)
+                    nc.vector.scalar_tensor_tensor(
+                        out=t[:, cols], in0=halves[a][:], scalar=mean_var[:, 0:1], in1=gb[:, cols],
+                        op0=ALU.subtract, op1=ALU.mult,
+                    )
+            else:
+                h = work.tile([P, H], F32, name="h", tag="h", bufs=4)
+                sums = small.tile([P, 2], F32, name="sums")
+                for a in range(2):
+                    nc.scalar.activation(
+                        out=h[:, BANK * a : BANK * a + BANK], in_=halves[a][:], func=ACT.Identity,
+                        accum_out=sums[:, a : a + 1],
+                    )
+                neg_mean = small.tile([P, 1], F32, name="neg_mean")
+                parts = small.tile([P, 2], F32, name="parts")
+                nc.scalar.activation(out=parts[:], in_=sums[:], func=ACT.Identity, scale=-1.0 / H, accum_out=neg_mean[:])
+                sum_sq = small.tile([P, 1], F32, name="sum_sq")
+                nc.scalar.activation(out=junk[:], in_=h[:], func=ACT.Square, bias=neg_mean[:], accum_out=sum_sq[:])
+                nc.scalar.activation(out=var_eps[:], in_=sum_sq[:], func=ACT.Identity, scale=1.0 / H, bias=eps_col[:])
+                nc.vector.scalar_tensor_tensor(
+                    out=t[:], in0=h[:], scalar=neg_mean[:], in1=gb[:, 0:H], op0=ALU.add, op1=ALU.mult
+                )
+            rstd[i] = small.tile([P, 1], F32, name="rstd")
+            nc.gpsimd.tensor_tensor(out=rstd[i][:], in0=var_eps[:], in1=neg_half[:], op=ALU.pow)
+            centred[i] = t
+
+        def finish(i):
+            c = chunk_of[i]
+            n = CHUNKS[c]
+            o = work.tile([P, H], F32, name="o", tag="o", bufs=4)
+            nc.vector.scalar_tensor_tensor(
+                out=o[:], in0=centred[i][:], scalar=rstd[i][:], in1=gb[:, H : 2 * H], op0=ALU.mult, op1=ALU.add
+            )
+            rows_c = out[P * starts[c] : P * (starts[c] + n), :].rearrange("(p r) h -> p r h", r=n)
+            nc.sync.dma_start(out=rows_c[:, i - starts[c], :], in_=o[:])
+
+        prepare_x(0, nc.scalar.copy)
+        prepare_x(1, nc.scalar.copy)
+        prepare_x(2, nc.vector.tensor_copy)
+        produce(0, range(NJ))
+        spread_g_beta()
+        produce(1, range(NJ))
+        for i in range(NT):
+            c = chunk_of[i]
+            n = CHUNKS[c]
+            r = i - starts[c]
+            if r == 0 and c + 3 < len(CHUNKS):
+                prepare_x(c + 3, nc.vector.tensor_copy if c + 3 in XV else nc.scalar.copy)
+            if c + 2 < len(CHUNKS):
+                produce(c + 2, range(NJ * r // n, NJ * (r + 1) // n))
+            centre(i)
+            if i >= 2:
+                finish(i - 2)
+        finish(NT - 2)
+        finish(NT - 1)

@@ -19,210 +19,396 @@ FLOPS = 2 * B * D * H
 NT = B // P
 NJ = H // P
 BANK = 512
-CHUNKS = (2, 2, 2, 2, 2, 2, 2, 2)
-VLIM = 12
-XV = (2,)
-W_VECTOR_COLS = 336
+R = 2
+NB = P * R
+NC = NT // R
+QC = H // 4
+M_CHUNKS = (6, 7)
 
 
 def tile_evidentialhead_pa_kernel(tc, x, W1, b1, g, beta, out):
     nc = tc.nc
-    starts = [sum(CHUNKS[:c]) for c in range(len(CHUNKS))]
-    chunk_of = [c for c, n in enumerate(CHUNKS) for r in range(n)]
     with ExitStack() as ctx:
+        ctx.enter_context(tc.manual_schedule())
         const = ctx.enter_context(tc.tile_pool(name="const", bufs=1))
         work = ctx.enter_context(tc.tile_pool(name="work", bufs=2))
         small = ctx.enter_context(tc.tile_pool(name="small", bufs=6))
-        psum = ctx.enter_context(tc.psum_pool(name="psum", bufs=8))
+        acc_pool = ctx.enter_context(tc.psum_pool(name="acc_pool", bufs=2))
+        x_pool = ctx.enter_context(tc.psum_pool(name="x_pool", bufs=2))
+        h_pool = ctx.enter_context(tc.psum_pool(name="h_pool", bufs=4))
 
-        def bank(name):
-            return psum.tile([P, BANK], F32, name=name, tag="bank")
+        vectors = const.tile([P, 3, P], BF16, name="vectors")
+        nc.vector.memset(vectors[:].rearrange("p v m -> p (v m)").bitcast(I32), 0)
+        w_raw = {}
 
-        rows = const.tile([P, 2 * H + P], BF16, name="rows")
-        nc.vector.memset(rows[:].bitcast(I32), 0)
-        ones = const.tile([P, P], BF16, name="ones")
-        nc.vector.memset(ones[:], 1.0)
-        neg_half = const.tile([P, 1], F32, name="neg_half")
-        nc.vector.memset(neg_half[:], -0.5)
-        eps_col = const.tile([P, 1], F32, name="eps_col")
-        nc.vector.memset(eps_col[:], EPS)
-        ident = const.tile([P, P], F32, name="ident")
-        make_identity(nc, ident[:])
-        warm = const.tile([P, 1], F32, name="warm")
-        nc.scalar.activation(out=warm[:], in_=neg_half[:], func=ACT.Silu)
-        nc.scalar.dma_start(out=rows[0:1, 0:H], in_=g.unsqueeze(0))
-        nc.scalar.dma_start(out=rows[0:1, H : 2 * H], in_=beta.unsqueeze(0))
-        nc.scalar.dma_start(out=rows[0:NJ, 2 * H : 2 * H + P], in_=b1.rearrange("(j m) -> j m", m=P))
-
-        w_raw = const.tile([P, 8, H], BF16, name="w_raw")
-        for gi in range(2):
+        def load_w(half, gi):
+            raw = const.tile([P, 4, BANK], BF16, name="w_raw%d%d" % (half, gi))
             nc.sync.dma_start(
-                out=w_raw[:, 4 * gi : 4 * gi + 4, :],
-                in_=W1[512 * gi : 512 * gi + 512, :].rearrange("(p e) c -> p e c", e=4),
+                out=raw[:],
+                in_=W1[512 * gi : 512 * gi + 512, BANK * half : BANK * half + BANK].rearrange("(p e) c -> p e c", e=4),
             )
+            w_raw[half, gi] = raw
+
         x_raw = []
-        for c, n in enumerate(CHUNKS):
-            xc = const.tile([P, n, D], BF16, name="x_raw%d" % c)
-            nc.sync.dma_start(
-                out=xc[:], in_=x[P * starts[c] : P * (starts[c] + n), :].rearrange("(p r) k -> p r k", r=n)
-            )
+
+        def load_x(c):
+            xc = const.tile([P, R, D], BF16, name="x_raw%d" % c)
+            nc.sync.dma_start(out=xc[:], in_=x[NB * c : NB * (c + 1), :].rearrange("(p r) k -> p r k", r=R))
             x_raw.append(xc)
 
-        b1_rows = const.tile([P, P], F32, name="b1_rows")
-        nc.vector.tensor_copy(out=b1_rows[:], in_=rows[:, 2 * H : 2 * H + P])
-        b1_bank = bank("b1_bank")
-        nc.tensor.transpose(b1_bank[:, 0:P], b1_rows[:], ident[:])
+        load_w(0, 0)
+        for v, vector in enumerate((b1, g, beta)):
+            nc.sync.dma_start(out=vectors[0:NJ, v, :], in_=vector.rearrange("(j m) -> j m", m=P))
+        load_x(0)
+        load_w(0, 1)
+        load_w(1, 0)
+        load_w(1, 1)
+        for c in range(1, NC):
+            load_x(c)
+
+        ident_bf16 = const.tile([P, P], BF16, name="ident_bf16")
+        make_identity(nc, ident_bf16[:])
+        ident = const.tile([P, P], F32, name="ident")
+        make_identity(nc, ident[:])
+        neg_half = const.tile([P, 1], F32, name="neg_half")
+        nc.vector.memset(neg_half[:], -0.5)
+        half_eps = const.tile([P, 1], F32, name="half_eps")
+        nc.vector.memset(half_eps[:], EPS / 2)
+        eps_col = const.tile([P, 1], F32, name="eps_col")
+        nc.vector.memset(eps_col[:], EPS)
+        warm = const.tile([P, 1], F32, name="warm")
+        nc.scalar.activation(out=warm[:], in_=neg_half[:], func=ACT.Silu)
+
         b1_col = const.tile([P, NJ], F32, name="b1_col")
-        nc.vector.tensor_copy(out=b1_col[:], in_=b1_bank[:, 0:NJ])
 
-        w_grouped = const.tile([P, 2, H, 4], BF16, name="w_grouped", align_bytes=64)
-        w_codes = const.tile([P, 2, H], U32, name="w_codes", align_bytes=64)
-        w_scales = const.tile([P, 2, H], U8, name="w_scales", align_bytes=64)
-        for gi in range(2):
-            for lo in (0, BANK):
-                cut = lo + W_VECTOR_COLS
-                for copy, a, b in ((nc.vector.tensor_copy, lo, cut), (nc.scalar.copy, cut, lo + BANK)):
-                    copy(
-                        out=w_grouped[:, gi, a:b, :].rearrange("p (c i) t -> p c t i", i=4),
-                        in_=w_raw[:, 4 * gi : 4 * gi + 4, a:b].rearrange("p t (c i) -> p c t i", i=4),
-                    )
-            for lo in (0, BANK):
-                nc.vector.quantize_mx(
-                    out=w_codes[:, gi, lo : lo + BANK].bitcast(FP8X4),
-                    scales=w_scales[:, gi, lo : lo + BANK],
-                    in_=w_grouped[:, gi, lo : lo + BANK, :].rearrange("p c t -> p (c t)"),
-                )
+        def spread_b1():
+            turned = h_pool.tile([P, P], BF16, name="b1_turned", tag="h_half")
+            nc.tensor.transpose(turned[:], vectors[:, 0, :], ident_bf16[:])
+            nc.vector.tensor_copy(out=b1_col[:], in_=turned[:, 0:NJ])
 
+        w_grouped = {}
+        w_codes = {}
+        w_scales = {}
+
+        def group_w(k, gi, copy):
+            grouped = const.tile([P, QC, 4], BF16, name="w_grouped%d%d" % (k, gi), align_bytes=64)
+            raw = w_raw[k // 2, gi][:, :, QC * (k % 2) : QC * (k % 2) + QC]
+            copy(
+                out=grouped[:].rearrange("p (c i) t -> p c t i", i=4), in_=raw.rearrange("p t (c i) -> p c t i", i=4)
+            )
+            w_grouped[k, gi] = grouped
+
+        def quantise_w(k, gi):
+            codes = const.tile([P, QC], U32, name="w_codes%d%d" % (k, gi), align_bytes=64)
+            scales = const.tile([P, QC], U8, name="w_scales%d%d" % (k, gi), align_bytes=64)
+            nc.vector.quantize_mx(
+                out=codes[:].bitcast(FP8X4), scales=scales[:], in_=w_grouped[k, gi][:].rearrange("p c t -> p (c t)")
+            )
+            w_codes[k, gi] = codes
+            w_scales[k, gi] = scales
+
+        x_turned = {}
+        x_grouped = {}
         x_codes = {}
         x_scales = {}
 
-        def prepare_x(c, copy):
-            n = CHUNKS[c]
-            nb = P * n
-            grouped = work.tile([P, 8 * nb], BF16, name="x_grouped", tag="x_grouped", bufs=3, align_bytes=64)
-            for r in range(n):
-                turned = bank("x_turned")
-                words = x_raw[c][:, r, :].bitcast(F32)
-                for w in range(4):
-                    first = 256 * (w // 2) + w % 2
-                    nc.tensor.transpose(turned[:, P * w : P * w + P], words[:, first : first + 255 : 2], ident[:])
-                copy(
-                    out=grouped[:].bitcast(F32).rearrange("p (g b u) -> p g b u", g=2, u=2)[:, :, P * r : P * r + P, :],
-                    in_=turned[:].rearrange("p (g u b) -> p g b u", g=2, u=2),
-                )
-            x_codes[c] = const.tile([P, 2 * nb], U32, name="x_codes%d" % c, align_bytes=64)
-            x_scales[c] = const.tile([P, 2 * nb], U8, name="x_scales%d" % c, align_bytes=64)
-            nc.vector.quantize_mx(out=x_codes[c][:].bitcast(FP8X4), scales=x_scales[c][:], in_=grouped[:])
+        def turn_x(i):
+            c, r = divmod(i, R)
+            if i in (2, 3):
+                turned = h_pool.tile([P, BANK], F32, name="x_turned", tag="h_half")
+            else:
+                turned = x_pool.tile([P, BANK], F32, name="x_turned", tag="x_turned")
+            words = x_raw[c][:, r, :].bitcast(F32)
+            for w in range(4):
+                first = 256 * (w // 2) + w % 2
+                nc.tensor.transpose(turned[:, P * w : P * w + P], words[:, first : first + 255 : 2], ident[:])
+            x_turned[i] = turned
+
+        def group_x(i, copy):
+            c, r = divmod(i, R)
+            if r == 0:
+                x_grouped[c] = work.tile([P, 8 * NB], BF16, name="x_grouped", tag="x_grouped", bufs=3, align_bytes=64)
+            copy(
+                out=x_grouped[c][:].bitcast(F32).rearrange("p (g b u) -> p g b u", g=2, u=2)[:, :, P * r : P * r + P, :],
+                in_=x_turned[i][:].rearrange("p (g u b) -> p g b u", g=2, u=2),
+            )
+
+        def quantise_x(c):
+            x_codes[c] = const.tile([P, 2 * NB], U32, name="x_codes%d" % c, align_bytes=64)
+            x_scales[c] = const.tile([P, 2 * NB], U8, name="x_scales%d" % c, align_bytes=64)
+            nc.vector.quantize_mx(out=x_codes[c][:].bitcast(FP8X4), scales=x_scales[c][:], in_=x_grouped[c][:])
 
         hT = {}
+        accs = {}
 
-        def produce(c, js):
-            nb = P * CHUNKS[c]
-            for j in js:
-                if j == 0:
-                    hT[c] = work.tile([P, NJ, nb], F32, name="hT", tag="hT", bufs=4)
-                acc = bank("acc")
+        def multiply(c, js):
+            acc = acc_pool.tile([P, BANK], F32, name="acc", tag="acc")
+            for s, j in enumerate(js):
+                k, jj = divmod(j, 2)
                 for gi in range(2):
                     nc.tensor.matmul_mx(
-                        out=acc[:, 0:nb],
-                        lhsT=w_codes[:, gi, P * j : P * j + P].bitcast(FP8X4),
-                        lhsT_scale=w_scales[:, gi, P * j : P * j + P],
-                        rhs=x_codes[c][:, nb * gi : nb * gi + nb].bitcast(FP8X4),
-                        rhs_scale=x_scales[c][:, nb * gi : nb * gi + nb],
+                        out=acc[:, NB * s : NB * s + NB],
+                        lhsT=w_codes[k, gi][:, P * jj : P * jj + P].bitcast(FP8X4),
+                        lhsT_scale=w_scales[k, gi][:, P * jj : P * jj + P],
+                        rhs=x_codes[c][:, NB * gi : NB * gi + NB].bitcast(FP8X4),
+                        rhs_scale=x_scales[c][:, NB * gi : NB * gi + NB],
                         start=(gi == 0),
                         stop=(gi == 1),
                     )
+                accs[c, j] = acc[:, NB * s : NB * s + NB]
+
+        def silu(c, js):
+            for j in js:
+                if j == 0:
+                    hT[c] = work.tile([P, NJ, NB], F32, name="hT", tag="hT", bufs=4)
                 nc.scalar.activation(
-                    out=hT[c][:, j, :], in_=acc[:, 0:nb], func=ACT.Silu, bias=b1_col[:, j : j + 1], scale=1.0
+                    out=hT[c][:, j, :], in_=accs[c, j], func=ACT.Silu, bias=b1_col[:, j : j + 1], scale=1.0
                 )
 
-        gb = const.tile([P, 2 * H], F32, name="gb")
+        gb = const.tile([P, 2 * H], BF16, name="gb")
 
-        def spread_g_beta():
-            for q in range(4):
-                spread = bank("spread")
+        def spread_g_beta(v, copy):
+            spread = h_pool.tile([P, H], BF16, name="spread", tag="h_half")
+            for j in range(NJ):
                 nc.tensor.matmul(
-                    out=spread[:], lhsT=ones[:], rhs=rows[:, BANK * q : BANK * q + BANK], start=True, stop=True
+                    out=spread[:, P * j : P * j + P],
+                    lhsT=ident_bf16[:, j : j + 1].to_broadcast([P, P]),
+                    rhs=vectors[:, 1 + v, :],
+                    start=True,
+                    stop=True,
                 )
-                nc.vector.tensor_copy(out=gb[:, BANK * q : BANK * q + BANK], in_=spread[:])
+            copy(out=gb[:, H * v : H * v + H], in_=spread[:])
 
         junk = const.tile([P, H], F32, name="junk")
+        halves = {}
+        sums = {}
         centred = {}
         rstd = {}
 
-        def centre(i):
-            c = chunk_of[i]
-            r = i - starts[c]
-            halves = []
+        def turn_h(i):
+            c, r = divmod(i, R)
+            halves[i] = []
             for a in range(2):
-                half = bank("h_half")
+                half = h_pool.tile([P, BANK], F32, name="h_half", tag="h_half")
                 for jj in range(4):
                     nc.tensor.transpose(half[:, P * jj : P * jj + P], hT[c][:, 4 * a + jj, P * r : P * r + P], ident[:])
-                halves.append(half)
+                halves[i].append(half)
+
+        shift = {}
+        var_eps = {}
+        h_rows = {}
+        sum_sq = {}
+
+        def statistics_v(i):
+            stats = small.tile([P, 2, 6], F32, name="stats")
+            for a in range(2):
+                nc.vector.bn_stats(out=stats[:, a, :], in_=halves[i][a][:])
+            mean_var = small.tile([P, 2], F32, name="mean_var")
+            nc.vector.bn_aggr(out=mean_var[:], in_=stats[:].rearrange("p a s -> p (a s)"))
+            shift[i] = mean_var[:, 0:1]
+            var_eps[i] = small.tile([P, 1], F32, name="var_eps")
+            nc.gpsimd.tensor_scalar(
+                out=var_eps[i][:], in0=mean_var[:, 1:2], scalar1=1.0, scalar2=EPS, op0=ALU.mult, op1=ALU.add
+            )
+
+        def centre_v(i, op):
             t = work.tile([P, H], F32, name="centred", tag="centred", bufs=5)
-            var_eps = small.tile([P, 1], F32, name="var_eps")
-            if (i == 0 or i % 2 == 1) and i < VLIM:
-                stats = small.tile([P, 2, 6], F32, name="stats")
-                for a in range(2):
-                    nc.vector.bn_stats(out=stats[:, a, :], in_=halves[a][:])
-                mean_var = small.tile([P, 2], F32, name="mean_var")
-                nc.vector.bn_aggr(out=mean_var[:], in_=stats[:].rearrange("p a s -> p (a s)"))
-                nc.gpsimd.tensor_scalar(
-                    out=var_eps[:], in0=mean_var[:, 1:2], scalar1=1.0, scalar2=EPS, op0=ALU.mult, op1=ALU.add
-                )
-                for a in range(2):
-                    cols = slice(BANK * a, BANK * a + BANK)
-                    nc.vector.scalar_tensor_tensor(
-                        out=t[:, cols], in0=halves[a][:], scalar=mean_var[:, 0:1], in1=gb[:, cols],
-                        op0=ALU.subtract, op1=ALU.mult,
-                    )
-            else:
-                h = work.tile([P, H], F32, name="h", tag="h", bufs=4)
-                sums = small.tile([P, 2], F32, name="sums")
-                for a in range(2):
-                    nc.scalar.activation(
-                        out=h[:, BANK * a : BANK * a + BANK], in_=halves[a][:], func=ACT.Identity,
-                        accum_out=sums[:, a : a + 1],
-                    )
-                neg_mean = small.tile([P, 1], F32, name="neg_mean")
-                parts = small.tile([P, 2], F32, name="parts")
-                nc.scalar.activation(out=parts[:], in_=sums[:], func=ACT.Identity, scale=-1.0 / H, accum_out=neg_mean[:])
-                sum_sq = small.tile([P, 1], F32, name="sum_sq")
-                nc.scalar.activation(out=junk[:], in_=h[:], func=ACT.Square, bias=neg_mean[:], accum_out=sum_sq[:])
-                nc.scalar.activation(out=var_eps[:], in_=sum_sq[:], func=ACT.Identity, scale=1.0 / H, bias=eps_col[:])
+            for a in range(2):
+                cols = slice(BANK * a, BANK * a + BANK)
                 nc.vector.scalar_tensor_tensor(
-                    out=t[:], in0=h[:], scalar=neg_mean[:], in1=gb[:, 0:H], op0=ALU.add, op1=ALU.mult
+                    out=t[:, cols], in0=halves[i][a][:], scalar=shift[i], in1=gb[:, cols], op0=op, op1=ALU.mult
                 )
-            rstd[i] = small.tile([P, 1], F32, name="rstd")
-            nc.gpsimd.tensor_tensor(out=rstd[i][:], in0=var_eps[:], in1=neg_half[:], op=ALU.pow)
             centred[i] = t
 
-        def finish(i):
-            c = chunk_of[i]
-            n = CHUNKS[c]
-            o = work.tile([P, H], F32, name="o", tag="o", bufs=4)
-            nc.vector.scalar_tensor_tensor(
-                out=o[:], in0=centred[i][:], scalar=rstd[i][:], in1=gb[:, H : 2 * H], op0=ALU.mult, op1=ALU.add
-            )
-            rows_c = out[P * starts[c] : P * (starts[c] + n), :].rearrange("(p r) h -> p r h", r=n)
-            nc.sync.dma_start(out=rows_c[:, i - starts[c], :], in_=o[:])
+        def leave_s(i):
+            h = work.tile([P, H], F32, name="h", tag="h", bufs=3)
+            totals = small.tile([P, 2], F32, name="totals")
+            for a in range(2):
+                nc.scalar.activation(
+                    out=h[:, BANK * a : BANK * a + BANK], in_=halves[i][a][:], func=ACT.Identity,
+                    accum_out=totals[:, a : a + 1],
+                )
+            h_rows[i] = h
+            sums[i] = totals
 
-        prepare_x(0, nc.scalar.copy)
-        prepare_x(1, nc.scalar.copy)
-        prepare_x(2, nc.vector.tensor_copy)
-        produce(0, range(NJ))
-        spread_g_beta()
-        produce(1, range(NJ))
-        for i in range(NT):
-            c = chunk_of[i]
-            n = CHUNKS[c]
-            r = i - starts[c]
-            if r == 0 and c + 3 < len(CHUNKS):
-                prepare_x(c + 3, nc.vector.tensor_copy if c + 3 in XV else nc.scalar.copy)
-            if c + 2 < len(CHUNKS):
-                produce(c + 2, range(NJ * r // n, NJ * (r + 1) // n))
-            centre(i)
-            if i >= 2:
-                finish(i - 2)
-        finish(NT - 2)
-        finish(NT - 1)
+        def mean_s(i):
+            neg_mean = small.tile([P, 1], F32, name="neg_mean")
+            parts = small.tile([P, 2], F32, name="parts")
+            nc.scalar.activation(
+                out=parts[:], in_=sums[i][:], func=ACT.Identity, scale=-1.0 / H, accum_out=neg_mean[:]
+            )
+            shift[i] = neg_mean[:]
+
+        def squares_s(i):
+            sum_sq[i] = small.tile([P, 1], F32, name="sum_sq")
+            nc.scalar.activation(
+                out=junk[:], in_=h_rows[i][:], func=ACT.Square, bias=shift[i], accum_out=sum_sq[i][:]
+            )
+
+        def variance_s(i):
+            var_eps[i] = small.tile([P, 1], F32, name="var_eps")
+            nc.scalar.activation(
+                out=var_eps[i][:], in_=sum_sq[i][:], func=ACT.Identity, scale=1.0 / H, bias=eps_col[:]
+            )
+
+        def centre_s(i):
+            t = work.tile([P, H], F32, name="centred", tag="centred", bufs=5)
+            nc.vector.scalar_tensor_tensor(
+                out=t[:], in0=h_rows[i][:], scalar=shift[i], in1=gb[:, 0:H], op0=ALU.add, op1=ALU.mult
+            )
+            centred[i] = t
+
+        def sum_h(i):
+            c, r = divmod(i, R)
+            eighth = x_pool.tile([P, P], F32, name="h_eighth", tag="x_turned")
+            for j in range(NJ):
+                nc.tensor.matmul(
+                    out=eighth[:], lhsT=hT[c][:, j, P * r : P * r + P], rhs=ident[:],
+                    start=(j == 0), stop=(j == NJ - 1), is_transpose=True,
+                )
+            sums[i] = eighth
+
+        def mean_m(i):
+            neg_mean = small.tile([P, 1], F32, name="neg_mean")
+            nc.scalar.activation(
+                out=junk[:, 0:P], in_=sums[i][:], func=ACT.Identity, scale=-1.0 / H, accum_out=neg_mean[:]
+            )
+            shift[i] = neg_mean[:]
+
+        def squares_m(i):
+            halves_sq = small.tile([P, 2], F32, name="halves_sq")
+            for a in range(2):
+                nc.scalar.activation(
+                    out=junk[:, BANK * a : BANK * a + BANK], in_=halves[i][a][:], func=ACT.Square,
+                    bias=shift[i], accum_out=halves_sq[:, a : a + 1],
+                )
+            sum_sq[i] = halves_sq
+
+        def variance_m(i):
+            var_eps[i] = small.tile([P, 1], F32, name="var_eps")
+            parts = small.tile([P, 2], F32, name="parts")
+            nc.scalar.activation(
+                out=parts[:], in_=sum_sq[i][:], func=ACT.Identity, scale=1.0 / H, bias=half_eps[:], accum_out=var_eps[i][:]
+            )
+
+        def invert(i):
+            rstd[i] = small.tile([P, 1], F32, name="rstd")
+            nc.gpsimd.tensor_tensor(out=rstd[i][:], in0=var_eps[i][:], in1=neg_half[:], op=ALU.pow)
+
+        def finish(i, pieces=1):
+            c, r = divmod(i, R)
+            o = work.tile([P, H], F32, name="o", tag="o", bufs=4)
+            rows_c = out[NB * c : NB * (c + 1), :].rearrange("(p r) h -> p r h", r=R)
+            width = H // pieces
+            for k in range(pieces):
+                cols = slice(width * k, width * k + width)
+                nc.vector.scalar_tensor_tensor(
+                    out=o[:, cols], in0=centred[i][:, cols], scalar=rstd[i][:], in1=gb[:, H + width * k : H + width * k + width],
+                    op0=ALU.mult, op1=ALU.add,
+                )
+                nc.sync.dma_start(out=rows_c[:, r, cols], in_=o[:, cols])
+
+        def pair(c, k):
+            return c, range(2 * k, 2 * k + 2)
+
+        def exit_x(i):
+            group_x(i, nc.scalar.copy)
+
+        vcopy = nc.vector.tensor_copy
+        scopy = nc.scalar.copy
+        spread_b1()
+        group_w(0, 0, vcopy)
+        group_w(1, 0, scopy)
+        quantise_w(0, 0)
+        spread_g_beta(0, scopy)
+        spread_g_beta(1, vcopy)
+        for i in (0, 1):
+            turn_x(i)
+            exit_x(i)
+        group_w(0, 1, vcopy)
+        group_w(1, 1, scopy)
+        quantise_w(0, 1)
+        quantise_w(1, 0)
+        group_w(2, 0, vcopy)
+        quantise_x(0)
+        multiply(*pair(0, 0))
+        group_w(3, 0, scopy)
+        group_w(2, 1, vcopy)
+        quantise_w(1, 1)
+        silu(*pair(0, 0))
+        multiply(*pair(0, 1))
+        quantise_w(2, 0)
+        quantise_w(2, 1)
+        for i in (2, 3):
+            turn_x(i)
+        silu(*pair(0, 1))
+        exit_x(2)
+        multiply(*pair(0, 2))
+        group_w(3, 1, vcopy)
+        quantise_w(3, 0)
+        quantise_w(3, 1)
+        for i in (4, 5):
+            turn_x(i)
+        group_x(3, vcopy)
+        silu(*pair(0, 2))
+        multiply(*pair(0, 3))
+        quantise_x(1)
+        group_x(4, vcopy)
+        silu(*pair(0, 3))
+        multiply(*pair(1, 0))
+        exit_x(5)
+        turn_h(1)
+        turn_h(0)
+        multiply(*pair(1, 1))
+
+        for c in range(NC):
+            v, s = 2 * c, 2 * c + 1
+            more = c + 1 < NC
+            mm = c in M_CHUNKS
+            xs = (2 * c + 6, 2 * c + 7) if c + 3 < NC else ()
+            if more:
+                silu(*pair(c + 1, 0))
+                multiply(*pair(c + 1, 2))
+            leave_s(s)
+            if mm:
+                mean_m(v)
+                squares_m(v)
+                variance_m(v)
+            if more:
+                silu(*pair(c + 1, 1))
+                multiply(*pair(c + 1, 3))
+            mean_s(s)
+            squares_s(s)
+            for i in xs:
+                turn_x(i)
+            if c + 2 < NC:
+                quantise_x(c + 2)
+            if mm:
+                finish(s - 2)
+            else:
+                statistics_v(v)
+            invert(v)
+            centre_v(v, ALU.add if mm else ALU.subtract)
+            if c > 0 and not mm:
+                finish(s - 2)
+            centre_s(s)
+            finish(v)
+            if more:
+                silu(*pair(c + 1, 2))
+            for i in xs[:1]:
+                exit_x(i)
+            if more:
+                if c + 2 < NC:
+                    multiply(*pair(c + 2, 0))
+                silu(*pair(c + 1, 3))
+                turn_h(s + 2)
+                if c + 2 < NC:
+                    multiply(*pair(c + 2, 1))
+                if c + 1 in M_CHUNKS:
+                    sum_h(v + 2)
+                turn_h(v + 2)
+            variance_s(s)
+            invert(s)
+            for i in xs[1:]:
+                exit_x(i)
+        finish(NT - 1, 2)

@@ -19,11 +19,11 @@ FLOPS = 2 * B * D * H
 NT = B // P
 NJ = H // P
 BANK = 512
-R = 2
-NB = P * R
-NC = NT // R
+LOAD = 2
+CHUNKS = ((0, 1), (2, 3), (4, 5), (6, 7), (8, 9), (10, 11), (12, 13), (14,), (15,))
+NC = len(CHUNKS)
 QC = H // 4
-M_CHUNKS = (6, 7)
+KINDS = ("VS", "VS", "VS", "VS", "VS", "VS", "MM", "M", "M")
 
 
 def tile_evidentialhead_pa_kernel(tc, x, W1, b1, g, beta, out):
@@ -49,12 +49,14 @@ def tile_evidentialhead_pa_kernel(tc, x, W1, b1, g, beta, out):
             )
             w_raw[half, gi] = raw
 
+        place = {i: (c, r, P * len(tiles)) for c, tiles in enumerate(CHUNKS) for r, i in enumerate(tiles)}
         x_raw = []
 
-        def load_x(c):
-            xc = const.tile([P, R, D], BF16, name="x_raw%d" % c)
-            nc.sync.dma_start(out=xc[:], in_=x[NB * c : NB * (c + 1), :].rearrange("(p r) k -> p r k", r=R))
-            x_raw.append(xc)
+        def load_x(d):
+            xd = const.tile([P, LOAD, D], BF16, name="x_raw%d" % d)
+            rows_d = x[P * LOAD * d : P * LOAD * (d + 1), :]
+            nc.sync.dma_start(out=xd[:], in_=rows_d.rearrange("(p r) k -> p r k", r=LOAD))
+            x_raw.append(xd)
 
         load_w(0, 0)
         for v, vector in enumerate((b1, g, beta)):
@@ -63,8 +65,8 @@ def tile_evidentialhead_pa_kernel(tc, x, W1, b1, g, beta, out):
         load_w(0, 1)
         load_w(1, 0)
         load_w(1, 1)
-        for c in range(1, NC):
-            load_x(c)
+        for d in range(1, NT // LOAD):
+            load_x(d)
 
         ident_bf16 = const.tile([P, P], BF16, name="ident_bf16")
         make_identity(nc, ident_bf16[:])
@@ -107,62 +109,78 @@ def tile_evidentialhead_pa_kernel(tc, x, W1, b1, g, beta, out):
             w_codes[k, gi] = codes
             w_scales[k, gi] = scales
 
+        def keep_warm(count):
+            idle = h_pool.tile([P, BANK], F32, name="idle", tag="h_half")
+            for k in range(count):
+                nc.tensor.matmul(out=idle[:], lhsT=ident_bf16[:], rhs=w_raw[0, 0][:, k, :], start=True, stop=True)
+
         x_turned = {}
         x_grouped = {}
         x_codes = {}
         x_scales = {}
 
         def turn_x(i):
-            c, r = divmod(i, R)
             if i in (2, 3):
                 turned = h_pool.tile([P, BANK], F32, name="x_turned", tag="h_half")
             else:
                 turned = x_pool.tile([P, BANK], F32, name="x_turned", tag="x_turned")
-            words = x_raw[c][:, r, :].bitcast(F32)
+            words = x_raw[i // LOAD][:, i % LOAD, :].bitcast(F32)
             for w in range(4):
                 first = 256 * (w // 2) + w % 2
                 nc.tensor.transpose(turned[:, P * w : P * w + P], words[:, first : first + 255 : 2], ident[:])
             x_turned[i] = turned
 
         def group_x(i, copy):
-            c, r = divmod(i, R)
+            c, r, nb = place[i]
             if r == 0:
-                x_grouped[c] = work.tile([P, 8 * NB], BF16, name="x_grouped", tag="x_grouped", bufs=3, align_bytes=64)
+                x_grouped[c] = work.tile([P, 8 * nb], BF16, name="x_grouped", tag="x_grouped", bufs=3, align_bytes=64)
             copy(
                 out=x_grouped[c][:].bitcast(F32).rearrange("p (g b u) -> p g b u", g=2, u=2)[:, :, P * r : P * r + P, :],
                 in_=x_turned[i][:].rearrange("p (g u b) -> p g b u", g=2, u=2),
             )
 
         def quantise_x(c):
-            x_codes[c] = const.tile([P, 2 * NB], U32, name="x_codes%d" % c, align_bytes=64)
-            x_scales[c] = const.tile([P, 2 * NB], U8, name="x_scales%d" % c, align_bytes=64)
+            nb = P * len(CHUNKS[c])
+            x_codes[c] = const.tile([P, 2 * nb], U32, name="x_codes%d" % c, align_bytes=64)
+            x_scales[c] = const.tile([P, 2 * nb], U8, name="x_scales%d" % c, align_bytes=64)
             nc.vector.quantize_mx(out=x_codes[c][:].bitcast(FP8X4), scales=x_scales[c][:], in_=x_grouped[c][:])
 
         hT = {}
         accs = {}
 
-        def multiply(c, js):
+        groups = []
+        for c, tiles in enumerate(CHUNKS):
+            width = BANK // (P * len(tiles))
+            groups.extend((c, range(j, j + width)) for j in range(0, NJ, width))
+
+        def multiply(n):
+            if n >= len(groups):
+                return
+            c, js = groups[n]
+            nb = P * len(CHUNKS[c])
             acc = acc_pool.tile([P, BANK], F32, name="acc", tag="acc")
             for s, j in enumerate(js):
                 k, jj = divmod(j, 2)
                 for gi in range(2):
                     nc.tensor.matmul_mx(
-                        out=acc[:, NB * s : NB * s + NB],
+                        out=acc[:, nb * s : nb * s + nb],
                         lhsT=w_codes[k, gi][:, P * jj : P * jj + P].bitcast(FP8X4),
                         lhsT_scale=w_scales[k, gi][:, P * jj : P * jj + P],
-                        rhs=x_codes[c][:, NB * gi : NB * gi + NB].bitcast(FP8X4),
-                        rhs_scale=x_scales[c][:, NB * gi : NB * gi + NB],
+                        rhs=x_codes[c][:, nb * gi : nb * gi + nb].bitcast(FP8X4),
+                        rhs_scale=x_scales[c][:, nb * gi : nb * gi + nb],
                         start=(gi == 0),
                         stop=(gi == 1),
                     )
-                accs[c, j] = acc[:, NB * s : NB * s + NB]
+            accs[n] = acc
 
-        def silu(c, js):
-            for j in js:
+        def silu(n):
+            c, js = groups[n]
+            nb = P * len(CHUNKS[c])
+            for s, j in enumerate(js):
                 if j == 0:
-                    hT[c] = work.tile([P, NJ, NB], F32, name="hT", tag="hT", bufs=4)
+                    hT[c] = work.tile([P, NJ, nb], F32, name="hT", tag="hT", bufs=4)
                 nc.scalar.activation(
-                    out=hT[c][:, j, :], in_=accs[c, j], func=ACT.Silu, bias=b1_col[:, j : j + 1], scale=1.0
+                    out=hT[c][:, j, :], in_=accs[n][:, nb * s : nb * s + nb], func=ACT.Silu, bias=b1_col[:, j : j + 1], scale=1.0
                 )
 
         gb = const.tile([P, 2 * H], BF16, name="gb")
@@ -186,7 +204,7 @@ def tile_evidentialhead_pa_kernel(tc, x, W1, b1, g, beta, out):
         rstd = {}
 
         def turn_h(i):
-            c, r = divmod(i, R)
+            c, r, nb = place[i]
             halves[i] = []
             for a in range(2):
                 half = h_pool.tile([P, BANK], F32, name="h_half", tag="h_half")
@@ -259,7 +277,7 @@ def tile_evidentialhead_pa_kernel(tc, x, W1, b1, g, beta, out):
             centred[i] = t
 
         def sum_h(i):
-            c, r = divmod(i, R)
+            c, r, nb = place[i]
             eighth = x_pool.tile([P, P], F32, name="h_eighth", tag="x_turned")
             for j in range(NJ):
                 nc.tensor.matmul(
@@ -296,9 +314,9 @@ def tile_evidentialhead_pa_kernel(tc, x, W1, b1, g, beta, out):
             nc.gpsimd.tensor_tensor(out=rstd[i][:], in0=var_eps[i][:], in1=neg_half[:], op=ALU.pow)
 
         def finish(i, pieces=1):
-            c, r = divmod(i, R)
             o = work.tile([P, H], F32, name="o", tag="o", bufs=4)
-            rows_c = out[NB * c : NB * (c + 1), :].rearrange("(p r) h -> p r h", r=R)
+            d, r = divmod(i, LOAD)
+            rows_d = out[P * LOAD * d : P * LOAD * (d + 1), :].rearrange("(p r) h -> p r h", r=LOAD)
             width = H // pieces
             for k in range(pieces):
                 cols = slice(width * k, width * k + width)
@@ -306,10 +324,7 @@ def tile_evidentialhead_pa_kernel(tc, x, W1, b1, g, beta, out):
                     out=o[:, cols], in0=centred[i][:, cols], scalar=rstd[i][:], in1=gb[:, H + width * k : H + width * k + width],
                     op0=ALU.mult, op1=ALU.add,
                 )
-                nc.sync.dma_start(out=rows_c[:, r, cols], in_=o[:, cols])
-
-        def pair(c, k):
-            return c, range(2 * k, 2 * k + 2)
+                nc.sync.dma_start(out=rows_d[:, r, cols], in_=o[:, cols])
 
         def exit_x(i):
             group_x(i, nc.scalar.copy)
@@ -318,97 +333,117 @@ def tile_evidentialhead_pa_kernel(tc, x, W1, b1, g, beta, out):
         scopy = nc.scalar.copy
         spread_b1()
         group_w(0, 0, vcopy)
-        group_w(1, 0, scopy)
-        quantise_w(0, 0)
+        group_w(1, 0, vcopy)
         spread_g_beta(0, scopy)
-        spread_g_beta(1, vcopy)
+        quantise_w(0, 0)
+        quantise_w(1, 0)
         for i in (0, 1):
             turn_x(i)
             exit_x(i)
+        spread_g_beta(1, scopy)
+        keep_warm(3)
         group_w(0, 1, vcopy)
-        group_w(1, 1, scopy)
+        group_w(1, 1, vcopy)
         quantise_w(0, 1)
-        quantise_w(1, 0)
-        group_w(2, 0, vcopy)
         quantise_x(0)
-        multiply(*pair(0, 0))
-        group_w(3, 0, scopy)
-        group_w(2, 1, vcopy)
         quantise_w(1, 1)
-        silu(*pair(0, 0))
-        multiply(*pair(0, 1))
+        multiply(0)
+        multiply(1)
+        group_w(3, 0, scopy)
+        group_w(2, 0, vcopy)
+        group_w(2, 1, vcopy)
+        silu(0)
         quantise_w(2, 0)
         quantise_w(2, 1)
         for i in (2, 3):
             turn_x(i)
-        silu(*pair(0, 1))
-        exit_x(2)
-        multiply(*pair(0, 2))
+        silu(1)
+        multiply(2)
         group_w(3, 1, vcopy)
+        exit_x(2)
+        exit_x(3)
         quantise_w(3, 0)
         quantise_w(3, 1)
+        silu(2)
+        multiply(3)
+        quantise_x(1)
         for i in (4, 5):
             turn_x(i)
-        group_x(3, vcopy)
-        silu(*pair(0, 2))
-        multiply(*pair(0, 3))
-        quantise_x(1)
+        silu(3)
+        multiply(4)
         group_x(4, vcopy)
-        silu(*pair(0, 3))
-        multiply(*pair(1, 0))
-        exit_x(5)
-        turn_h(1)
+        group_x(5, vcopy)
         turn_h(0)
-        multiply(*pair(1, 1))
+        turn_h(1)
+        multiply(5)
 
+        n = 4
         for c in range(NC):
-            v, s = 2 * c, 2 * c + 1
-            more = c + 1 < NC
-            mm = c in M_CHUNKS
-            xs = (2 * c + 6, 2 * c + 7) if c + 3 < NC else ()
-            if more:
-                silu(*pair(c + 1, 0))
-                multiply(*pair(c + 1, 2))
-            leave_s(s)
-            if mm:
-                mean_m(v)
-                squares_m(v)
-                variance_m(v)
-            if more:
-                silu(*pair(c + 1, 1))
-                multiply(*pair(c + 1, 3))
-            mean_s(s)
-            squares_s(s)
-            for i in xs:
-                turn_x(i)
-            if c + 2 < NC:
-                quantise_x(c + 2)
-            if mm:
-                finish(s - 2)
-            else:
-                statistics_v(v)
-            invert(v)
-            centre_v(v, ALU.add if mm else ALU.subtract)
-            if c > 0 and not mm:
-                finish(s - 2)
-            centre_s(s)
-            finish(v)
-            if more:
-                silu(*pair(c + 1, 2))
-            for i in xs[:1]:
-                exit_x(i)
-            if more:
-                if c + 2 < NC:
-                    multiply(*pair(c + 2, 0))
-                silu(*pair(c + 1, 3))
-                turn_h(s + 2)
-                if c + 2 < NC:
-                    multiply(*pair(c + 2, 1))
-                if c + 1 in M_CHUNKS:
-                    sum_h(v + 2)
-                turn_h(v + 2)
-            variance_s(s)
-            invert(s)
-            for i in xs[1:]:
-                exit_x(i)
-        finish(NT - 1, 2)
+            tiles = CHUNKS[c]
+            kinds = KINDS[c]
+            nxt = CHUNKS[c + 1] if c + 1 < NC else ()
+            nkinds = KINDS[c + 1] if c + 1 < NC else ""
+            xs = tuple(i for i in (2 * c + 6, 2 * c + 7) if i < NT)
+            ready = (c + 2,) if c < 5 else (7, 8) if c == 5 else ()
+            count = 2 * len(nxt)
+            slots = []
+            for i, kind in zip(tiles, kinds):
+                if kind == "S":
+                    slots.append([(leave_s, i)])
+                    slots.append([(mean_s, i), (squares_s, i)])
+                    slots.append([(variance_s, i)])
+                if kind == "M":
+                    slots.append([(mean_m, i)])
+                    slots.append([(squares_m, i)])
+                    slots.append([(variance_m, i)])
+            if kinds == "MM":
+                slots = [slots[0], slots[1], slots[2] + slots[3], slots[4], slots[5]]
+            if kinds == "MS":
+                slots = [slots[3], slots[0] + slots[1], slots[2] + slots[4], slots[5]]
+            for k, i in enumerate(xs):
+                slots.append([(exit_x, i)])
+            first_m = kinds[0] == "M"
+            if ready:
+                for d in ready:
+                    quantise_x(d)
+            if c > 0 and first_m:
+                finish(tiles[0] - 1)
+            if kinds[0] == "V":
+                statistics_v(tiles[0])
+                invert(tiles[0])
+                centre_v(tiles[0], ALU.subtract)
+                if c > 0:
+                    finish(tiles[0] - 1)
+            q = 0
+            while q < count or slots:
+                if q < count:
+                    silu(n + q)
+                    if q + 1 < count:
+                        multiply(n + q + 2)
+                    q += 1
+                if slots:
+                    for f, i in slots.pop(0):
+                        f(i)
+                        if f is squares_m:
+                            centre_v(i, ALU.add)
+                            if i == tiles[-1] and len(tiles) == 2:
+                                finish(tiles[0])
+                        if f is mean_s:
+                            centre_s(i)
+                            finish(tiles[0])
+                        if f in (variance_m, variance_s):
+                            invert(i)
+                if q == 2:
+                    for i in xs:
+                        turn_x(i)
+            order = list(zip(nxt, nkinds))
+            if nkinds in ("VS", "MS", "VM"):
+                order.reverse()
+            for k, (i, kind) in enumerate(order):
+                if kind == "M":
+                    sum_h(i)
+                turn_h(i)
+                if k == 0:
+                    multiply(n + count + 1)
+            n += count
+        finish(NT - 1, 4)

@@ -23,6 +23,8 @@ LOAD = 2
 CHUNKS = ((0, 1), (2, 3), (4, 5), (6, 7), (8, 9), (10, 11), (12, 13), (14,), (15,))
 NC = len(CHUNKS)
 QC = H // 4
+XV0 = ()
+XV1 = ()
 KINDS = ("VS", "VS", "VS", "VS", "VS", "VS", "MM", "M", "M")
 
 
@@ -173,10 +175,12 @@ def tile_evidentialhead_pa_kernel(tc, x, W1, b1, g, beta, out):
                     )
             accs[n] = acc
 
-        def silu(n):
+        def silu(n, part=None):
             c, js = groups[n]
             nb = P * len(CHUNKS[c])
             for s, j in enumerate(js):
+                if part is not None and s * 2 // len(js) != part:
+                    continue
                 if j == 0:
                     hT[c] = work.tile([P, NJ, nb], F32, name="hT", tag="hT", bufs=4)
                 nc.scalar.activation(
@@ -185,7 +189,16 @@ def tile_evidentialhead_pa_kernel(tc, x, W1, b1, g, beta, out):
 
         gb = const.tile([P, 2 * H], BF16, name="gb")
 
+        spreads = {}
+
         def spread_g_beta(v, copy):
+            gather_g_beta(v)
+            copy(out=gb[:, H * v : H * v + H], in_=spreads[v][:])
+
+        def keep_g_beta(v, copy):
+            copy(out=gb[:, H * v : H * v + H], in_=spreads[v][:])
+
+        def gather_g_beta(v):
             spread = h_pool.tile([P, H], BF16, name="spread", tag="h_half")
             for j in range(NJ):
                 nc.tensor.matmul(
@@ -195,7 +208,7 @@ def tile_evidentialhead_pa_kernel(tc, x, W1, b1, g, beta, out):
                     start=True,
                     stop=True,
                 )
-            copy(out=gb[:, H * v : H * v + H], in_=spread[:])
+            spreads[v] = spread
 
         junk = const.tile([P, H], F32, name="junk")
         halves = {}
@@ -213,6 +226,7 @@ def tile_evidentialhead_pa_kernel(tc, x, W1, b1, g, beta, out):
                 halves[i].append(half)
 
         shift = {}
+        bn = {}
         var_eps = {}
         h_rows = {}
         sum_sq = {}
@@ -221,8 +235,11 @@ def tile_evidentialhead_pa_kernel(tc, x, W1, b1, g, beta, out):
             stats = small.tile([P, 2, 6], F32, name="stats")
             for a in range(2):
                 nc.vector.bn_stats(out=stats[:, a, :], in_=halves[i][a][:])
+            bn[i] = stats
+
+        def aggregate_v(i):
             mean_var = small.tile([P, 2], F32, name="mean_var")
-            nc.vector.bn_aggr(out=mean_var[:], in_=stats[:].rearrange("p a s -> p (a s)"))
+            nc.vector.bn_aggr(out=mean_var[:], in_=bn[i][:].rearrange("p a s -> p (a s)"))
             shift[i] = mean_var[:, 0:1]
             var_eps[i] = small.tile([P, 1], F32, name="var_eps")
             nc.gpsimd.tensor_scalar(
@@ -331,17 +348,16 @@ def tile_evidentialhead_pa_kernel(tc, x, W1, b1, g, beta, out):
 
         vcopy = nc.vector.tensor_copy
         scopy = nc.scalar.copy
-        spread_b1()
         group_w(0, 0, vcopy)
         group_w(1, 0, vcopy)
-        spread_g_beta(0, scopy)
+        spread_b1()
         quantise_w(0, 0)
         quantise_w(1, 0)
+        spread_g_beta(0, vcopy)
         for i in (0, 1):
             turn_x(i)
             exit_x(i)
-        spread_g_beta(1, scopy)
-        keep_warm(3)
+        keep_warm(2)
         group_w(0, 1, vcopy)
         group_w(1, 1, vcopy)
         quantise_w(0, 1)
@@ -359,6 +375,7 @@ def tile_evidentialhead_pa_kernel(tc, x, W1, b1, g, beta, out):
             turn_x(i)
         silu(1)
         multiply(2)
+        gather_g_beta(1)
         group_w(3, 1, vcopy)
         exit_x(2)
         exit_x(3)
@@ -373,6 +390,7 @@ def tile_evidentialhead_pa_kernel(tc, x, W1, b1, g, beta, out):
         multiply(4)
         group_x(4, vcopy)
         group_x(5, vcopy)
+        keep_g_beta(1, vcopy)
         turn_h(0)
         turn_h(1)
         multiply(5)
@@ -386,64 +404,70 @@ def tile_evidentialhead_pa_kernel(tc, x, W1, b1, g, beta, out):
             xs = tuple(i for i in (2 * c + 6, 2 * c + 7) if i < NT)
             ready = (c + 2,) if c < 5 else (7, 8) if c == 5 else ()
             count = 2 * len(nxt)
-            slots = []
-            for i, kind in zip(tiles, kinds):
-                if kind == "S":
-                    slots.append([(leave_s, i)])
-                    slots.append([(mean_s, i), (squares_s, i)])
-                    slots.append([(variance_s, i)])
-                if kind == "M":
-                    slots.append([(mean_m, i)])
-                    slots.append([(squares_m, i)])
-                    slots.append([(variance_m, i)])
-            if kinds == "MM":
-                slots = [slots[0], slots[1], slots[2] + slots[3], slots[4], slots[5]]
-            if kinds == "MS":
-                slots = [slots[3], slots[0] + slots[1], slots[2] + slots[4], slots[5]]
-            for k, i in enumerate(xs):
-                slots.append([(exit_x, i)])
-            first_m = kinds[0] == "M"
-            if ready:
+            if kinds == "VS":
+                v, s = tiles
+                statistics_v(v)
+                if c > 0:
+                    finish(v - 1)
+                aggregate_v(v)
                 for d in ready:
                     quantise_x(d)
-            if c > 0 and first_m:
+                invert(v)
+                centre_v(v, ALU.subtract)
+                silu(n)
+                multiply(n + 2)
+                leave_s(s)
+                silu(n + 1, 0)
+                mean_s(s)
+                silu(n + 1, 1)
+                multiply(n + 3)
+                squares_s(s)
+                centre_s(s)
+                finish(v)
+                for i in xs:
+                    turn_x(i)
+                silu(n + 2)
+                multiply(n + 4)
+                for i in xs[:1]:
+                    group_x(i, vcopy if c in XV0 else scopy)
+                silu(n + 3)
+                variance_s(s)
+                invert(s)
+                for i in xs[1:]:
+                    group_x(i, vcopy if c in XV1 else scopy)
+            else:
                 finish(tiles[0] - 1)
-            if kinds[0] == "V":
-                statistics_v(tiles[0])
-                invert(tiles[0])
-                centre_v(tiles[0], ALU.subtract)
-                if c > 0:
-                    finish(tiles[0] - 1)
-            q = 0
-            while q < count or slots:
-                if q < count:
-                    silu(n + q)
-                    if q + 1 < count:
-                        multiply(n + q + 2)
-                    q += 1
-                if slots:
-                    for f, i in slots.pop(0):
+                for d in ready:
+                    quantise_x(d)
+                slots = []
+                for i in tiles:
+                    slots.extend(((mean_m, i), (squares_m, i), (variance_m, i)))
+                q = 0
+                while q < count or slots:
+                    if q < count:
+                        silu(n + q)
+                        if q + 1 < count:
+                            multiply(n + q + 2)
+                        q += 1
+                    for f, i in slots[:1 if q < count else 6]:
                         f(i)
                         if f is squares_m:
                             centre_v(i, ALU.add)
-                            if i == tiles[-1] and len(tiles) == 2:
+                            if i != tiles[0]:
                                 finish(tiles[0])
-                        if f is mean_s:
-                            centre_s(i)
-                            finish(tiles[0])
-                        if f in (variance_m, variance_s):
+                        if f is variance_m:
                             invert(i)
-                if q == 2:
-                    for i in xs:
-                        turn_x(i)
+                    slots = slots[1 if q < count else 6 :]
             order = list(zip(nxt, nkinds))
-            if nkinds in ("VS", "MS", "VM"):
+            if nkinds == "VS":
                 order.reverse()
+            if "M" in nkinds:
+                multiply(n + count + 1)
             for k, (i, kind) in enumerate(order):
                 if kind == "M":
                     sum_h(i)
                 turn_h(i)
-                if k == 0:
+                if k == (len(order) - 1 if c == 0 else 0) and "M" not in nkinds:
                     multiply(n + count + 1)
             n += count
         finish(NT - 1, 4)

@@ -384,16 +384,14 @@ def tile_evidentialhead_pa_kernel(tc, x, W1, b1, g, beta, out):
         silu(2)
         multiply(3)
         quantise_x(1)
-        for i in (4, 5):
-            turn_x(i)
         silu(3)
         multiply(4)
-        group_x(4, vcopy)
-        group_x(5, vcopy)
         keep_g_beta(1, vcopy)
         turn_h(0)
         turn_h(1)
         multiply(5)
+        for i in (4, 5):
+            turn_x(i)
 
         n = 4
         for c in range(NC):
@@ -410,10 +408,15 @@ def tile_evidentialhead_pa_kernel(tc, x, W1, b1, g, beta, out):
                 if c > 0:
                     finish(v - 1)
                 aggregate_v(v)
-                for d in ready:
-                    quantise_x(d)
+                if c > 0:
+                    for d in ready:
+                        quantise_x(d)
                 invert(v)
                 centre_v(v, ALU.subtract)
+                if c == 0:
+                    for i in (4, 5):
+                        group_x(i, vcopy)
+                    quantise_x(2)
                 silu(n)
                 multiply(n + 2)
                 leave_s(s)
@@ -467,7 +470,7 @@ def tile_evidentialhead_pa_kernel(tc, x, W1, b1, g, beta, out):
                 if kind == "M":
                     sum_h(i)
                 turn_h(i)
-                if k == (len(order) - 1 if c == 0 else 0) and "M" not in nkinds:
+                if k == len(order) - 1 and "M" not in nkinds:
                     multiply(n + count + 1)
             n += count
         finish(NT - 1, 4)

@@ -23,8 +23,6 @@ LOAD = 2
 CHUNKS = ((0, 1), (2, 3), (4, 5), (6, 7), (8, 9), (10, 11), (12, 13), (14,), (15,))
 NC = len(CHUNKS)
 QC = H // 4
-XV0 = ()
-XV1 = ()
 KINDS = ("VS", "VS", "VS", "VS", "VS", "VS", "MM", "M", "M")
 
 
@@ -286,6 +284,12 @@ def tile_evidentialhead_pa_kernel(tc, x, W1, b1, g, beta, out):
                 out=var_eps[i][:], in_=sum_sq[i][:], func=ACT.Identity, scale=1.0 / H, bias=eps_col[:]
             )
 
+        def variance_on_vector(i):
+            var_eps[i] = small.tile([P, 1], F32, name="var_eps")
+            nc.vector.tensor_scalar(
+                out=var_eps[i][:], in0=sum_sq[i][:], scalar1=1.0 / H, scalar2=EPS, op0=ALU.mult, op1=ALU.add
+            )
+
         def centre_s(i):
             t = work.tile([P, H], F32, name="centred", tag="centred", bufs=5)
             nc.vector.scalar_tensor_tensor(
@@ -427,17 +431,21 @@ def tile_evidentialhead_pa_kernel(tc, x, W1, b1, g, beta, out):
                 squares_s(s)
                 centre_s(s)
                 finish(v)
+                if c < 5:
+                    variance_on_vector(s)
+                    invert(s)
                 for i in xs:
                     turn_x(i)
                 silu(n + 2)
                 multiply(n + 4)
                 for i in xs[:1]:
-                    group_x(i, vcopy if c in XV0 else scopy)
+                    exit_x(i)
                 silu(n + 3)
-                variance_s(s)
-                invert(s)
+                if c == 5:
+                    variance_s(s)
+                    invert(s)
                 for i in xs[1:]:
-                    group_x(i, vcopy if c in XV1 else scopy)
+                    exit_x(i)
             else:
                 finish(tiles[0] - 1)
                 for d in ready:

@@ -64,8 +64,9 @@ def tile_evidentialhead_pa_kernel(tc, x, W1, b1, g, beta, out):
         load_x(0)
         load_w(0, 1)
         load_w(1, 0)
+        load_x(1)
         load_w(1, 1)
-        for d in range(1, NT // LOAD):
+        for d in range(2, NT // LOAD):
             load_x(d)
 
         ident_bf16 = const.tile([P, P], BF16, name="ident_bf16")
@@ -158,7 +159,10 @@ def tile_evidentialhead_pa_kernel(tc, x, W1, b1, g, beta, out):
                 return
             c, js = groups[n]
             nb = P * len(CHUNKS[c])
-            acc = acc_pool.tile([P, BANK], F32, name="acc", tag="acc")
+            if n in (2, 3):
+                acc = h_pool.tile([P, BANK], F32, name="acc", tag="h_half")
+            else:
+                acc = acc_pool.tile([P, BANK], F32, name="acc", tag="acc")
             for s, j in enumerate(js):
                 k, jj = divmod(j, 2)
                 for gi in range(2):
@@ -367,35 +371,36 @@ def tile_evidentialhead_pa_kernel(tc, x, W1, b1, g, beta, out):
         quantise_w(0, 1)
         quantise_x(0)
         quantise_w(1, 1)
+        group_w(3, 0, scopy)
+        for i in (2, 3):
+            turn_x(i)
+            exit_x(i)
         multiply(0)
         multiply(1)
-        group_w(3, 0, scopy)
         group_w(2, 0, vcopy)
         group_w(2, 1, vcopy)
         silu(0)
         quantise_w(2, 0)
         quantise_w(2, 1)
-        for i in (2, 3):
-            turn_x(i)
         silu(1)
         multiply(2)
-        gather_g_beta(1)
         group_w(3, 1, vcopy)
-        exit_x(2)
-        exit_x(3)
         quantise_w(3, 0)
         quantise_w(3, 1)
+        for i in (4, 5):
+            turn_x(i)
         silu(2)
         multiply(3)
         quantise_x(1)
+        for i in (4, 5):
+            group_x(i, vcopy)
+        quantise_x(2)
         silu(3)
         multiply(4)
-        keep_g_beta(1, vcopy)
         turn_h(0)
         turn_h(1)
         multiply(5)
-        for i in (4, 5):
-            turn_x(i)
+        gather_g_beta(1)
 
         n = 4
         for c in range(NC):
@@ -418,9 +423,7 @@ def tile_evidentialhead_pa_kernel(tc, x, W1, b1, g, beta, out):
                 invert(v)
                 centre_v(v, ALU.subtract)
                 if c == 0:
-                    for i in (4, 5):
-                        group_x(i, vcopy)
-                    quantise_x(2)
+                    keep_g_beta(1, vcopy)
                 silu(n)
                 multiply(n + 2)
                 leave_s(s)
@@ -439,13 +442,13 @@ def tile_evidentialhead_pa_kernel(tc, x, W1, b1, g, beta, out):
                 silu(n + 2)
                 multiply(n + 4)
                 for i in xs[:1]:
-                    exit_x(i)
+                    group_x(i, vcopy if c == 0 else scopy)
                 silu(n + 3)
                 if c == 5:
                     variance_s(s)
                     invert(s)
                 for i in xs[1:]:
-                    exit_x(i)
+                    group_x(i, vcopy if c == 0 else scopy)
             else:
                 finish(tiles[0] - 1)
                 for d in ready:

@@ -39,6 +39,8 @@ def tile_evidentialhead_pa_kernel(tc, x, W1, b1, g, beta, out):
 
         vectors = const.tile([P, 3, P], BF16, name="vectors")
         nc.vector.memset(vectors[:].rearrange("p v m -> p (v m)").bitcast(I32), 0)
+        zeros = const.tile([P, BANK], BF16, name="zeros")
+        nc.vector.memset(zeros[:].bitcast(I32), 0)
         w_raw = {}
 
         def load_w(half, gi):
@@ -113,7 +115,7 @@ def tile_evidentialhead_pa_kernel(tc, x, W1, b1, g, beta, out):
         def keep_warm(count):
             idle = h_pool.tile([P, BANK], F32, name="idle", tag="h_half")
             for k in range(count):
-                nc.tensor.matmul(out=idle[:], lhsT=ident_bf16[:], rhs=w_raw[0, 0][:, k, :], start=True, stop=True)
+                nc.tensor.matmul(out=idle[:], lhsT=zeros[:, 0:P], rhs=zeros[:], start=True, stop=True)
 
         x_turned = {}
         x_grouped = {}
@@ -356,6 +358,7 @@ def tile_evidentialhead_pa_kernel(tc, x, W1, b1, g, beta, out):
 
         vcopy = nc.vector.tensor_copy
         scopy = nc.scalar.copy
+        keep_warm(5)
         group_w(0, 0, vcopy)
         group_w(1, 0, vcopy)
         spread_b1()
@@ -365,7 +368,7 @@ def tile_evidentialhead_pa_kernel(tc, x, W1, b1, g, beta, out):
         for i in (0, 1):
             turn_x(i)
             exit_x(i)
-        keep_warm(2)
+        keep_warm(4)
         group_w(0, 1, vcopy)
         group_w(1, 1, vcopy)
         quantise_w(0, 1)

@@ -290,12 +290,6 @@ def tile_evidentialhead_pa_kernel(tc, x, W1, b1, g, beta, out):
                 out=var_eps[i][:], in_=sum_sq[i][:], func=ACT.Identity, scale=1.0 / H, bias=eps_col[:]
             )
 
-        def variance_on_vector(i):
-            var_eps[i] = small.tile([P, 1], F32, name="var_eps")
-            nc.vector.tensor_scalar(
-                out=var_eps[i][:], in0=sum_sq[i][:], scalar1=1.0 / H, scalar2=EPS, op0=ALU.mult, op1=ALU.add
-            )
-
         def centre_s(i):
             t = work.tile([P, H], F32, name="centred", tag="centred", bufs=5)
             nc.vector.scalar_tensor_tensor(
@@ -432,24 +426,20 @@ def tile_evidentialhead_pa_kernel(tc, x, W1, b1, g, beta, out):
                 leave_s(s)
                 silu(n + 1, 0)
                 mean_s(s)
+                for i in xs:
+                    turn_x(i)
                 silu(n + 1, 1)
                 multiply(n + 3)
                 squares_s(s)
                 centre_s(s)
                 finish(v)
-                if c < 5:
-                    variance_on_vector(s)
-                    invert(s)
-                for i in xs:
-                    turn_x(i)
                 silu(n + 2)
                 multiply(n + 4)
                 for i in xs[:1]:
-                    group_x(i, vcopy if c == 0 else scopy)
+                    exit_x(i)
                 silu(n + 3)
-                if c == 5:
-                    variance_s(s)
-                    invert(s)
+                variance_s(s)
+                invert(s)
                 for i in xs[1:]:
                     group_x(i, vcopy if c == 0 else scopy)
             else:

from contextlib import ExitStack

import concourse.mybir as mybir
from concourse.masks import make_identity

F32 = mybir.dt.float32
BF16 = mybir.dt.bfloat16
U32 = mybir.dt.uint32
U8 = mybir.dt.uint8
I32 = mybir.dt.int32
FP8X4 = mybir.dt.float8_e4m3fn_x4
ACT = mybir.ActivationFunctionType
ALU = mybir.AluOpType

P = 128
B, D, H = 2048, 1024, 1024
EPS = 1e-5
FLOPS = 2 * B * D * H
NT = B // P
NJ = H // P
BANK = 512
LOAD = 2
CHUNKS = ((0, 1), (2, 3), (4, 5), (6, 7), (8, 9), (10, 11), (12, 13), (14,), (15,))
NC = len(CHUNKS)
QC = H // 4
KINDS = ("VS", "VS", "VS", "VS", "VS", "VS", "MM", "M", "M")


def tile_evidentialhead_pa_kernel(tc, x, W1, b1, g, beta, out):
    nc = tc.nc
    with ExitStack() as ctx:
        ctx.enter_context(tc.manual_schedule())
        const = ctx.enter_context(tc.tile_pool(name="const", bufs=1))
        work = ctx.enter_context(tc.tile_pool(name="work", bufs=2))
        small = ctx.enter_context(tc.tile_pool(name="small", bufs=6))
        acc_pool = ctx.enter_context(tc.psum_pool(name="acc_pool", bufs=2))
        x_pool = ctx.enter_context(tc.psum_pool(name="x_pool", bufs=2))
        h_pool = ctx.enter_context(tc.psum_pool(name="h_pool", bufs=4))

        vectors = const.tile([P, 3, P], BF16, name="vectors")
        nc.vector.memset(vectors[:].rearrange("p v m -> p (v m)").bitcast(I32), 0)
        zeros = const.tile([P, BANK], BF16, name="zeros")
        nc.vector.memset(zeros[:].bitcast(I32), 0)
        w_raw = {}

        def load_w(half, gi):
            raw = const.tile([P, 4, BANK], BF16, name="w_raw%d%d" % (half, gi))
            nc.sync.dma_start(
                out=raw[:],
                in_=W1[512 * gi : 512 * gi + 512, BANK * half : BANK * half + BANK].rearrange("(p e) c -> p e c", e=4),
            )
            w_raw[half, gi] = raw

        place = {i: (c, r, P * len(tiles)) for c, tiles in enumerate(CHUNKS) for r, i in enumerate(tiles)}
        x_raw = []

        def load_x(d):
            xd = const.tile([P, LOAD, D], BF16, name="x_raw%d" % d)
            rows_d = x[P * LOAD * d : P * LOAD * (d + 1), :]
            nc.sync.dma_start(out=xd[:], in_=rows_d.rearrange("(p r) k -> p r k", r=LOAD))
            x_raw.append(xd)

        load_w(0, 0)
        for v, vector in enumerate((b1, g, beta)):
            nc.sync.dma_start(out=vectors[0:NJ, v, :], in_=vector.rearrange("(j m) -> j m", m=P))
        load_x(0)
        load_w(0, 1)
        load_w(1, 0)
        load_x(1)
        load_w(1, 1)
        for d in range(2, NT // LOAD):
            load_x(d)

        ident_bf16 = const.tile([P, P], BF16, name="ident_bf16")
        make_identity(nc, ident_bf16[:])
        ident = const.tile([P, P], F32, name="ident")
        make_identity(nc, ident[:])
        neg_half = const.tile([P, 1], F32, name="neg_half")
        nc.vector.memset(neg_half[:], -0.5)
        half_eps = const.tile([P, 1], F32, name="half_eps")
        nc.vector.memset(half_eps[:], EPS / 2)
        eps_col = const.tile([P, 1], F32, name="eps_col")
        nc.vector.memset(eps_col[:], EPS)
        warm = const.tile([P, 1], F32, name="warm")
        nc.scalar.activation(out=warm[:], in_=neg_half[:], func=ACT.Silu)

        b1_col = const.tile([P, NJ], F32, name="b1_col")

        def spread_b1():
            turned = h_pool.tile([P, P], BF16, name="b1_turned", tag="h_half")
            nc.tensor.transpose(turned[:], vectors[:, 0, :], ident_bf16[:])
            nc.vector.tensor_copy(out=b1_col[:], in_=turned[:, 0:NJ])

        w_grouped = {}
        w_codes = {}
        w_scales = {}

        def group_w(k, gi, copy):
            grouped = const.tile([P, QC, 4], BF16, name="w_grouped%d%d" % (k, gi), align_bytes=64)
            raw = w_raw[k // 2, gi][:, :, QC * (k % 2) : QC * (k % 2) + QC]
            copy(
                out=grouped[:].rearrange("p (c i) t -> p c t i", i=4), in_=raw.rearrange("p t (c i) -> p c t i", i=4)
            )
            w_grouped[k, gi] = grouped

        def quantise_w(k, gi):
            codes = const.tile([P, QC], U32, name="w_codes%d%d" % (k, gi), align_bytes=64)
            scales = const.tile([P, QC], U8, name="w_scales%d%d" % (k, gi), align_bytes=64)
            nc.vector.quantize_mx(
                out=codes[:].bitcast(FP8X4), scales=scales[:], in_=w_grouped[k, gi][:].rearrange("p c t -> p (c t)")
            )
            w_codes[k, gi] = codes
            w_scales[k, gi] = scales

        def keep_warm(count):
            idle = h_pool.tile([P, BANK], F32, name="idle", tag="h_half")
            for k in range(count):
                nc.tensor.matmul(out=idle[:], lhsT=zeros[:, 0:P], rhs=zeros[:], start=True, stop=True)

        x_turned = {}
        x_grouped = {}
        x_codes = {}
        x_scales = {}

        def turn_x(i):
            if i in (2, 3):
                turned = h_pool.tile([P, BANK], F32, name="x_turned", tag="h_half")
            else:
                turned = x_pool.tile([P, BANK], F32, name="x_turned", tag="x_turned")
            words = x_raw[i // LOAD][:, i % LOAD, :].bitcast(F32)
            for w in range(4):
                first = 256 * (w // 2) + w % 2
                nc.tensor.transpose(turned[:, P * w : P * w + P], words[:, first : first + 255 : 2], ident[:])
            x_turned[i] = turned

        def group_x(i, copy):
            c, r, nb = place[i]
            if r == 0:
                x_grouped[c] = work.tile([P, 8 * nb], BF16, name="x_grouped", tag="x_grouped", bufs=3, align_bytes=64)
            copy(
                out=x_grouped[c][:].bitcast(F32).rearrange("p (g b u) -> p g b u", g=2, u=2)[:, :, P * r : P * r + P, :],
                in_=x_turned[i][:].rearrange("p (g u b) -> p g b u", g=2, u=2),
            )

        def quantise_x(c):
            nb = P * len(CHUNKS[c])
            x_codes[c] = const.tile([P, 2 * nb], U32, name="x_codes%d" % c, align_bytes=64)
            x_scales[c] = const.tile([P, 2 * nb], U8, name="x_scales%d" % c, align_bytes=64)
            nc.vector.quantize_mx(out=x_codes[c][:].bitcast(FP8X4), scales=x_scales[c][:], in_=x_grouped[c][:])

        hT = {}
        accs = {}

        groups = []
        for c, tiles in enumerate(CHUNKS):
            width = BANK // (P * len(tiles))
            groups.extend((c, range(j, j + width)) for j in range(0, NJ, width))

        def multiply(n):
            if n >= len(groups):
                return
            c, js = groups[n]
            nb = P * len(CHUNKS[c])
            if n in (2, 3):
                acc = h_pool.tile([P, BANK], F32, name="acc", tag="h_half")
            else:
                acc = acc_pool.tile([P, BANK], F32, name="acc", tag="acc")
            for s, j in enumerate(js):
                k, jj = divmod(j, 2)
                for gi in range(2):
                    nc.tensor.matmul_mx(
                        out=acc[:, nb * s : nb * s + nb],
                        lhsT=w_codes[k, gi][:, P * jj : P * jj + P].bitcast(FP8X4),
                        lhsT_scale=w_scales[k, gi][:, P * jj : P * jj + P],
                        rhs=x_codes[c][:, nb * gi : nb * gi + nb].bitcast(FP8X4),
                        rhs_scale=x_scales[c][:, nb * gi : nb * gi + nb],
                        start=(gi == 0),
                        stop=(gi == 1),
                    )
            accs[n] = acc

        def silu(n, part=None):
            c, js = groups[n]
            nb = P * len(CHUNKS[c])
            for s, j in enumerate(js):
                if part is not None and s * 2 // len(js) != part:
                    continue
                if j == 0:
                    hT[c] = work.tile([P, NJ, nb], F32, name="hT", tag="hT", bufs=4)
                nc.scalar.activation(
                    out=hT[c][:, j, :], in_=accs[n][:, nb * s : nb * s + nb], func=ACT.Silu, bias=b1_col[:, j : j + 1], scale=1.0
                )

        gb = const.tile([P, 2 * H], BF16, name="gb")

        spreads = {}

        def spread_g_beta(v, copy):
            gather_g_beta(v)
            copy(out=gb[:, H * v : H * v + H], in_=spreads[v][:])

        def keep_g_beta(v, copy):
            copy(out=gb[:, H * v : H * v + H], in_=spreads[v][:])

        def gather_g_beta(v):
            spread = h_pool.tile([P, H], BF16, name="spread", tag="h_half")
            for j in range(NJ):
                nc.tensor.matmul(
                    out=spread[:, P * j : P * j + P],
                    lhsT=ident_bf16[:, j : j + 1].to_broadcast([P, P]),
                    rhs=vectors[:, 1 + v, :],
                    start=True,
                    stop=True,
                )
            spreads[v] = spread

        junk = const.tile([P, H], F32, name="junk")
        halves = {}
        sums = {}
        centred = {}
        rstd = {}

        def turn_h(i):
            c, r, nb = place[i]
            halves[i] = []
            for a in range(2):
                half = h_pool.tile([P, BANK], F32, name="h_half", tag="h_half")
                for jj in range(4):
                    nc.tensor.transpose(half[:, P * jj : P * jj + P], hT[c][:, 4 * a + jj, P * r : P * r + P], ident[:])
                halves[i].append(half)

        shift = {}
        bn = {}
        var_eps = {}
        h_rows = {}
        sum_sq = {}

        def statistics_v(i):
            stats = small.tile([P, 2, 6], F32, name="stats")
            for a in range(2):
                nc.vector.bn_stats(out=stats[:, a, :], in_=halves[i][a][:])
            bn[i] = stats

        def aggregate_v(i):
            mean_var = small.tile([P, 2], F32, name="mean_var")
            nc.vector.bn_aggr(out=mean_var[:], in_=bn[i][:].rearrange("p a s -> p (a s)"))
            shift[i] = mean_var[:, 0:1]
            var_eps[i] = small.tile([P, 1], F32, name="var_eps")
            nc.gpsimd.tensor_scalar(
                out=var_eps[i][:], in0=mean_var[:, 1:2], scalar1=1.0, scalar2=EPS, op0=ALU.mult, op1=ALU.add
            )

        def centre_v(i, op):
            t = work.tile([P, H], F32, name="centred", tag="centred", bufs=5)
            for a in range(2):
                cols = slice(BANK * a, BANK * a + BANK)
                nc.vector.scalar_tensor_tensor(
                    out=t[:, cols], in0=halves[i][a][:], scalar=shift[i], in1=gb[:, cols], op0=op, op1=ALU.mult
                )
            centred[i] = t

        def leave_s(i):
            h = work.tile([P, H], F32, name="h", tag="h", bufs=3)
            totals = small.tile([P, 2], F32, name="totals")
            for a in range(2):
                nc.scalar.activation(
                    out=h[:, BANK * a : BANK * a + BANK], in_=halves[i][a][:], func=ACT.Identity,
                    accum_out=totals[:, a : a + 1],
                )
            h_rows[i] = h
            sums[i] = totals

        def mean_s(i):
            neg_mean = small.tile([P, 1], F32, name="neg_mean")
            parts = small.tile([P, 2], F32, name="parts")
            nc.scalar.activation(
                out=parts[:], in_=sums[i][:], func=ACT.Identity, scale=-1.0 / H, accum_out=neg_mean[:]
            )
            shift[i] = neg_mean[:]

        def squares_s(i):
            sum_sq[i] = small.tile([P, 1], F32, name="sum_sq")
            nc.scalar.activation(
                out=junk[:], in_=h_rows[i][:], func=ACT.Square, bias=shift[i], accum_out=sum_sq[i][:]
            )

        def variance_s(i):
            var_eps[i] = small.tile([P, 1], F32, name="var_eps")
            nc.scalar.activation(
                out=var_eps[i][:], in_=sum_sq[i][:], func=ACT.Identity, scale=1.0 / H, bias=eps_col[:]
            )

        def centre_s(i):
            t = work.tile([P, H], F32, name="centred", tag="centred", bufs=5)
            nc.vector.scalar_tensor_tensor(
                out=t[:], in0=h_rows[i][:], scalar=shift[i], in1=gb[:, 0:H], op0=ALU.add, op1=ALU.mult
            )
            centred[i] = t

        def sum_h(i):
            c, r, nb = place[i]
            eighth = x_pool.tile([P, P], F32, name="h_eighth", tag="x_turned")
            for j in range(NJ):
                nc.tensor.matmul(
                    out=eighth[:], lhsT=hT[c][:, j, P * r : P * r + P], rhs=ident[:],
                    start=(j == 0), stop=(j == NJ - 1), is_transpose=True,
                )
            sums[i] = eighth

        def mean_m(i):
            neg_mean = small.tile([P, 1], F32, name="neg_mean")
            nc.scalar.activation(
                out=junk[:, 0:P], in_=sums[i][:], func=ACT.Identity, scale=-1.0 / H, accum_out=neg_mean[:]
            )
            shift[i] = neg_mean[:]

        def squares_m(i):
            halves_sq = small.tile([P, 2], F32, name="halves_sq")
            for a in range(2):
                nc.scalar.activation(
                    out=junk[:, BANK * a : BANK * a + BANK], in_=halves[i][a][:], func=ACT.Square,
                    bias=shift[i], accum_out=halves_sq[:, a : a + 1],
                )
            sum_sq[i] = halves_sq

        def variance_m(i):
            var_eps[i] = small.tile([P, 1], F32, name="var_eps")
            parts = small.tile([P, 2], F32, name="parts")
            nc.scalar.activation(
                out=parts[:], in_=sum_sq[i][:], func=ACT.Identity, scale=1.0 / H, bias=half_eps[:], accum_out=var_eps[i][:]
            )

        def invert(i):
            rstd[i] = small.tile([P, 1], F32, name="rstd")
            nc.gpsimd.tensor_tensor(out=rstd[i][:], in0=var_eps[i][:], in1=neg_half[:], op=ALU.pow)

        def finish(i, pieces=1):
            o = work.tile([P, H], F32, name="o", tag="o", bufs=4)
            d, r = divmod(i, LOAD)
            rows_d = out[P * LOAD * d : P * LOAD * (d + 1), :].rearrange("(p r) h -> p r h", r=LOAD)
            width = H // pieces
            for k in range(pieces):
                cols = slice(width * k, width * k + width)
                nc.vector.scalar_tensor_tensor(
                    out=o[:, cols], in0=centred[i][:, cols], scalar=rstd[i][:], in1=gb[:, H + width * k : H + width * k + width],
                    op0=ALU.mult, op1=ALU.add,
                )
                nc.sync.dma_start(out=rows_d[:, r, cols], in_=o[:, cols])

        def exit_x(i):
            group_x(i, nc.scalar.copy)

        vcopy = nc.vector.tensor_copy
        scopy = nc.scalar.copy
        keep_warm(5)
        group_w(0, 0, vcopy)
        group_w(1, 0, vcopy)
        spread_b1()
        quantise_w(0, 0)
        quantise_w(1, 0)
        spread_g_beta(0, vcopy)
        for i in (0, 1):
            turn_x(i)
            exit_x(i)
        keep_warm(4)
        group_w(0, 1, vcopy)
        group_w(1, 1, vcopy)
        quantise_w(0, 1)
        quantise_x(0)
        quantise_w(1, 1)
        group_w(3, 0, scopy)
        for i in (2, 3):
            turn_x(i)
            exit_x(i)
        multiply(0)
        multiply(1)
        group_w(2, 0, vcopy)
        group_w(2, 1, vcopy)
        silu(0)
        quantise_w(2, 0)
        quantise_w(2, 1)
        silu(1)
        multiply(2)
        group_w(3, 1, vcopy)
        quantise_w(3, 0)
        quantise_w(3, 1)
        for i in (4, 5):
            turn_x(i)
        silu(2)
        multiply(3)
        quantise_x(1)
        for i in (4, 5):
            group_x(i, vcopy)
        quantise_x(2)
        silu(3)
        multiply(4)
        turn_h(0)
        turn_h(1)
        multiply(5)
        gather_g_beta(1)

        n = 4
        for c in range(NC):
            tiles = CHUNKS[c]
            kinds = KINDS[c]
            nxt = CHUNKS[c + 1] if c + 1 < NC else ()
            nkinds = KINDS[c + 1] if c + 1 < NC else ""
            xs = tuple(i for i in (2 * c + 6, 2 * c + 7) if i < NT)
            ready = (c + 2,) if c < 5 else (7, 8) if c == 5 else ()
            count = 2 * len(nxt)
            if kinds == "VS":
                v, s = tiles
                statistics_v(v)
                if c > 0:
                    finish(v - 1)
                aggregate_v(v)
                if c > 0:
                    for d in ready:
                        quantise_x(d)
                invert(v)
                centre_v(v, ALU.subtract)
                if c == 0:
                    keep_g_beta(1, vcopy)
                silu(n)
                multiply(n + 2)
                leave_s(s)
                silu(n + 1, 0)
                mean_s(s)
                for i in xs:
                    turn_x(i)
                silu(n + 1, 1)
                multiply(n + 3)
                squares_s(s)
                centre_s(s)
                finish(v)
                silu(n + 2)
                multiply(n + 4)
                for i in xs[:1]:
                    exit_x(i)
                silu(n + 3)
                variance_s(s)
                invert(s)
                for i in xs[1:]:
                    group_x(i, vcopy if c == 0 else scopy)
            else:
                finish(tiles[0] - 1)
                for d in ready:
                    quantise_x(d)
                slots = []
                for i in tiles:
                    slots.extend(((mean_m, i), (squares_m, i), (variance_m, i)))
                q = 0
                while q < count or slots:
                    if q < count:
                        silu(n + q)
                        if q + 1 < count:
                            multiply(n + q + 2)
                        q += 1
                    for f, i in slots[:1 if q < count else 6]:
                        f(i)
                        if f is squares_m:
                            centre_v(i, ALU.add)
                            if i != tiles[0]:
                                finish(tiles[0])
                        if f is variance_m:
                            invert(i)
                    slots = slots[1 if q < count else 6 :]
            order = list(zip(nxt, nkinds))
            if nkinds == "VS":
                order.reverse()
            if "M" in nkinds:
                multiply(n + count + 1)
            for k, (i, kind) in enumerate(order):
                if kind == "M":
                    sum_h(i)
                turn_h(i)
                if k == len(order) - 1 and "M" not in nkinds:
                    multiply(n + count + 1)
            n += count
        finish(NT - 1, 4)
